import numpy as np
import ml_dtypes


def mxq(x, axis, fmt="e4m3"):
    dtype, down = {"e4m3": (ml_dtypes.float8_e4m3fn, 7), "e5m2": (ml_dtypes.float8_e5m2, 14)}[fmt]
    v = np.moveaxis(np.asarray(x, np.float32).astype(ml_dtypes.bfloat16).astype(np.float64), axis, -1)
    blocks = v.reshape(v.shape[:-1] + (-1, 32))
    amax = np.abs(blocks).max(-1, keepdims=True)
    byte = np.maximum(np.where(amax > 0, np.frexp(amax)[1] - 1 + 127, 0) - down, 1)
    scale = np.exp2(byte - 127.0)
    codes = (blocks / scale).astype(np.float32).astype(dtype).astype(np.float64)
    return np.moveaxis((codes * scale).reshape(v.shape), -1, axis)


WIDE = False


def mx_kscale(k):
    if not WIDE:
        return np.ones(k)
    levels = np.array([10, -10, 5, -5, 0])
    if k % 512:
        return np.exp2(np.random.permutation(np.resize(levels, k // 32))).repeat(32)
    a = np.empty((k // 512, 16))
    for p in range(k // 512):
        a[p, :8] = np.random.permutation(np.resize(levels, 8))
        for g in range(8):
            far = levels[np.abs(levels - a[p, g]) >= 10]
            a[p, g + 8] = far[np.random.randint(len(far))]
    return np.exp2(a.ravel()).repeat(32)


BF16 = ml_dtypes.bfloat16


def bf(x):
    return np.asarray(x, np.float32).astype(BF16)


def f64(x):
    return np.asarray(x).astype(np.float64)


N, NQ, G, KW = 1536, 512, 3, 3
P = KW - 1


def x_taps(x):
    return np.moveaxis(x.reshape(N, NQ, G, P), -1, 0).swapaxes(-1, -2).reshape(P, N * G, NQ)


def q_rows(q):
    return q.swapaxes(-1, -2).reshape(N * G, NQ)


def conv(xq, qq, W, b):
    wt = W.transpose(2, 1, 0)
    return (xq @ mxq(wt[:P], 1, "e4m3")).sum(0) + (qq @ mxq(wt[P], 0, "e4m3")) + b


def setup_inputs():
    s = mx_kscale(NQ)
    w = 1.0 / np.sqrt(KW * NQ)
    return {"x": bf(np.random.standard_normal((N, NQ, G * P)) * s[None, :, None]),
            "q2": bf(np.maximum(np.random.standard_normal((N, NQ, G)) * 0.9, 0.0) * s[None, :, None]),
            "q1": bf(np.random.standard_normal((N, NQ, G))),
            "W3": bf(np.random.standard_normal((NQ, NQ, KW)) * w / s[None, :, None]),
            "b3": bf(np.random.standard_normal(NQ) * 0.2)}


def reference(x, q2, q1, W3, b3):
    y = conv(mxq(x_taps(f64(x)), 2, "e4m3"), mxq(q_rows(f64(q2)), 1, "e4m3"), f64(W3), f64(b3))
    return np.maximum(y.reshape(N, G, NQ).swapaxes(-1, -2) + f64(q1), 0.0)

@@ -1,0 +1,218 @@
+from contextlib import ExitStack
+
+import concourse.mybir as mybir
+from concourse.masks import make_identity
+
+F32 = mybir.dt.float32
+BF16 = mybir.dt.bfloat16
+U32 = mybir.dt.uint32
+U8 = mybir.dt.uint8
+FP8X4 = mybir.dt.float8_e4m3fn_x4
+ADD = mybir.AluOpType.add
+RELU = mybir.ActivationFunctionType.Relu
+
+P = 128
+N, C, G, KW = 1536, 512, 3, 3
+O = 512
+NT = N // P
+PACK = 4
+OT = O // P
+NPOS = 9
+LAG = 2
+AHEAD = 4
+OC_POOL = 3
+FLOPS = 2 * N * G * O * C * KW
+
+
+def tile_quadjetresnetblock_pb_t_kernel(tc, x, q2, q1, W3, b3, out):
+    nc = tc.nc
+    x_t = x.rearrange("(i p) c j -> i p (c j)", p=P)
+    q2_t = q2.rearrange("(i p) c g -> i p (c g)", p=P)
+    q1_t = q1.rearrange("(i p) c g -> i p (c g)", p=P)
+    out_t = out.rearrange("(i p) o g -> i p (o g)", p=P)
+    w_t = W3.rearrange("(d p) c k -> d p (c k)", p=P)
+
+    with ExitStack() as ctx:
+        const = ctx.enter_context(tc.tile_pool(name="const", bufs=1))
+        xin = ctx.enter_context(tc.tile_pool(name="xin", bufs=AHEAD + 2))
+        work = ctx.enter_context(tc.tile_pool(name="work", bufs=LAG + 1))
+        res = ctx.enter_context(tc.tile_pool(name="res", bufs=6))
+        pst = ctx.enter_context(tc.psum_pool(name="pst", bufs=4))
+        psm = ctx.enter_context(tc.psum_pool(name="psm", bufs=4))
+        ctx.enter_context(tc.manual_schedule())
+
+        x_sb, q2_sb, q1_sb, grp, codes, scales, acc, ps = {}, {}, {}, {}, {}, {}, {}, {}
+
+        def load_xq(i):
+            x_sb[i] = xin.tile([P, C * 6], BF16, name="x_sb")
+            nc.sync.dma_start(out=x_sb[i][:], in_=x_t[i])
+            q2_sb[i] = xin.tile([P, C * G], BF16, name="q2_sb")
+            nc.sync.dma_start(out=q2_sb[i][:], in_=q2_t[i])
+
+        def load_q1(i):
+            q1_sb[i] = xin.tile([P, C * G], BF16, name="q1_sb")
+            nc.sync.dma_start(out=q1_sb[i][:], in_=q1_t[i])
+
+        def tx_x(i):
+            grp[i] = work.tile([P, NPOS, P, PACK], BF16, align_bytes=64, name="grp")
+            codes[i] = work.tile([P, NPOS, P], U32, align_bytes=64, name="codes")
+            scales[i] = work.tile([P, NPOS, P], U8, align_bytes=64, name="scales")
+            xw = x_sb[i][:].bitcast(F32).rearrange("p (i t g) -> p t g i", t=PACK, g=G)
+            banks = []
+            for g in range(G):
+                xt = pst.tile([P, PACK * P], F32, tag="tr", name="xt")
+                for t in range(PACK):
+                    nc.tensor.transpose(xt[:, t * P:(t + 1) * P], xw[:, t, g, :], ident_f[:])
+                banks.append(xt)
+            return banks
+
+        def ev_x(i, g, xt):
+            nc.scalar.copy(
+                out=grp[i][:, 2 * g:2 * g + 2, :, :],
+                in_=xt[:].bitcast(BF16).rearrange("p (t m k) -> p k m t", t=PACK, k=2),
+            )
+
+        def tx_triples(rows, a):
+            words = rows.bitcast(F32).rearrange("p (i a r) -> p a r i", a=2, r=3)
+            bank = pst.tile([P, PACK * P], F32, tag="tr", name="bank")
+            for r in range(3):
+                nc.tensor.transpose(bank[:, r * P:(r + 1) * P], words[:, a, r, :], ident_f[:])
+            return bank
+
+        def pick(bank, s):
+            off = [256 * ((3 * e + s) // 2) + (3 * e + s) % 2 for e in range(2)]
+            step = off[1] - off[0]
+            flat = bank[:].bitcast(BF16)[:, off[0]:off[0] + 2 * step]
+            cols = flat.rearrange("p (e b) -> p e b", e=2)[:, :, 0:2 * P]
+            return cols.rearrange("p e (j s) -> p j e s", s=2)[:, :, :, 0]
+
+        def ev_q(i, a, bank):
+            for g in range(G):
+                nc.vector.tensor_copy(out=grp[i][:, 6 + g, :, 2 * a:2 * a + 2], in_=pick(bank, g))
+
+        def quant(i, p0, npos):
+            nc.vector.quantize_mx(
+                out=codes[i][:, p0:p0 + npos, :].rearrange("p a m -> p (a m)").bitcast(FP8X4),
+                scales=scales[i][:, p0:p0 + npos, :].rearrange("p a m -> p (a m)"),
+                in_=grp[i][:, p0:p0 + npos, :, :].rearrange("p a m u -> p (a m u)"),
+            )
+
+        def residual_part(engine, i, oc):
+            cols = slice(oc * P * G, (oc + 1) * P * G)
+            engine.tensor_tensor(
+                out=acc[i][:, cols].rearrange("p (o g) -> p o g", g=G),
+                in0=q1_sb[i][:, cols].rearrange("p (o g) -> p o g", g=G),
+                in1=b_bc[:, oc * P:(oc + 1) * P].unsqueeze(2).to_broadcast([P, P, G]),
+                op=ADD,
+            )
+
+        def residual(i):
+            acc[i] = res.tile([P, O * G], F32, name="acc")
+            for oc in range(OT):
+                residual_part(nc.gpsimd if oc < OC_POOL else nc.vector, i, oc)
+
+        def mm(i, oc):
+            ps[oc] = psm.tile([P, G, P], F32, tag="mm", name="ps")
+            for g in range(G):
+                for k in range(KW):
+                    pos = 2 * g + k if k < 2 else 6 + g
+                    nc.tensor.matmul_mx(
+                        out=ps[oc][:, g, :],
+                        lhsT=codes[i][:, pos, :].bitcast(FP8X4),
+                        lhsT_scale=scales[i][:, pos, :],
+                        rhs=w_codes[:, k, oc * P:(oc + 1) * P].bitcast(FP8X4),
+                        rhs_scale=w_scales[:, k, oc * P:(oc + 1) * P],
+                        start=(k == 0),
+                        stop=(k == KW - 1),
+                    )
+
+        def add(i, oc):
+            part = acc[i][:, oc * P * G:(oc + 1) * P * G].rearrange("p (o g) -> p o g", g=G)
+            nc.vector.tensor_tensor(out=part, in0=ps[oc][:].rearrange("p g o -> p o g"), in1=part, op=ADD)
+
+        def relu_store(i, oc0, oc1):
+            lo, hi = oc0 * P * G, oc1 * P * G
+            part = acc[i][:, lo:hi]
+            nc.scalar.activation(out=part, in_=part, func=RELU)
+            nc.scalar.dma_start(out=out_t[i][:, lo:hi], in_=part)
+
+        def prepare(i):
+            xb = tx_x(i)
+            for g in range(G):
+                ev_x(i, g, xb[g])
+            quant(i, 0, 4)
+            for a in range(2):
+                ev_q(i, a, tx_triples(q2_sb[i][:], a))
+            quant(i, 4, 4)
+            quant(i, 8, 1)
+
+        w_sb = const.tile([P, 4, C * KW], BF16)
+        for d in range(4):
+            nc.sync.dma_start(out=w_sb[:, d, :], in_=w_t[d])
+        b_bc = const.tile([P, O], BF16)
+        nc.scalar.dma_start(out=b_bc[:], in_=b3.partition_broadcast(P))
+        for i in range(LAG):
+            load_xq(i)
+        for i in range(LAG):
+            load_q1(i)
+        for i in range(LAG, AHEAD):
+            load_xq(i)
+            load_q1(i)
+        ident_f = const.tile([P, P], F32)
+        make_identity(nc, ident_f[:])
+
+        w_grp = const.tile([P, KW, O, PACK], BF16, align_bytes=64)
+        w_codes = const.tile([P, KW, O], U32, align_bytes=64)
+        w_scales = const.tile([P, KW, O], U8, align_bytes=64)
+        for d in range(4):
+            for a in range(2):
+                bank = tx_triples(w_sb[:, d, :], a)
+                for k in range(KW):
+                    dst = w_grp[:, k, d * P:(d + 1) * P, 2 * a:2 * a + 2]
+                    if a == 0:
+                        nc.vector.tensor_copy(out=dst, in_=pick(bank, k))
+                    else:
+                        nc.scalar.copy(out=dst, in_=pick(bank, k))
+        for k in range(KW):
+            nc.vector.quantize_mx(
+                out=w_codes[:, k, :].bitcast(FP8X4),
+                scales=w_scales[:, k, :],
+                in_=w_grp[:, k, :, :].rearrange("p o u -> p (o u)"),
+            )
+        for i in range(LAG):
+            prepare(i)
+            residual(i)
+
+        for i in range(NT):
+            nxt = i + LAG
+            more = nxt < NT
+            if i + AHEAD < NT:
+                load_xq(i + AHEAD)
+                load_q1(i + AHEAD)
+            if more:
+                residual(nxt)
+                xb = tx_x(nxt)
+                for g in range(G):
+                    ev_x(nxt, g, xb[g])
+            if i > 0:
+                add(i - 1, 2)
+                add(i - 1, 3)
+                relu_store(i - 1, 0, OT)
+            mm(i, 0)
+            mm(i, 1)
+            add(i, 0)
+            if more:
+                quant(nxt, 0, 4)
+            add(i, 1)
+            if more:
+                for a in range(2):
+                    ev_q(nxt, a, tx_triples(q2_sb[nxt][:], a))
+                quant(nxt, 4, 4)
+                quant(nxt, 8, 1)
+            mm(i, 2)
+            mm(i, 3)
+        relu_store(NT - 1, 0, 2)
+        add(NT - 1, 2)
+        relu_store(NT - 1, 2, 3)
+        add(NT - 1, 3)
+        relu_store(NT - 1, 3, 4)

@@ -18,9 +18,8 @@ NT = N // P
 PACK = 4
 OT = O // P
 NPOS = 9
-LAG = 2
-AHEAD = 4
-OC_POOL = 3
+RAW = 1
+AHEAD = 5
 FLOPS = 2 * N * G * O * C * KW
 
 
@@ -34,61 +33,66 @@ def tile_quadjetresnetblock_pb_t_kernel(tc, x, q2, q1, W3, b3, out):
 
     with ExitStack() as ctx:
         const = ctx.enter_context(tc.tile_pool(name="const", bufs=1))
-        xin = ctx.enter_context(tc.tile_pool(name="xin", bufs=AHEAD + 2))
-        work = ctx.enter_context(tc.tile_pool(name="work", bufs=LAG + 1))
-        res = ctx.enter_context(tc.tile_pool(name="res", bufs=6))
-        pst = ctx.enter_context(tc.psum_pool(name="pst", bufs=4))
-        psm = ctx.enter_context(tc.psum_pool(name="psm", bufs=4))
+        xin = ctx.enter_context(tc.tile_pool(name="xin", bufs=AHEAD + 1))
+        sep = ctx.enter_context(tc.tile_pool(name="sep", bufs=2))
+        work = ctx.enter_context(tc.tile_pool(name="work", bufs=2))
+        res = ctx.enter_context(tc.tile_pool(name="res", bufs=4))
+        pst = ctx.enter_context(tc.psum_pool(name="pst", bufs=5))
+        psm = ctx.enter_context(tc.psum_pool(name="psm", bufs=3))
         ctx.enter_context(tc.manual_schedule())
 
-        x_sb, q2_sb, q1_sb, grp, codes, scales, acc, ps = {}, {}, {}, {}, {}, {}, {}, {}
+        x_sb, q2_sb, q1_sb, xs, qs, grp, codes, scales, acc, ps = {}, {}, {}, {}, {}, {}, {}, {}, {}, {}
 
-        def load_xq(i):
+        def load(i):
             x_sb[i] = xin.tile([P, C * 6], BF16, name="x_sb")
             nc.sync.dma_start(out=x_sb[i][:], in_=x_t[i])
             q2_sb[i] = xin.tile([P, C * G], BF16, name="q2_sb")
             nc.sync.dma_start(out=q2_sb[i][:], in_=q2_t[i])
-
-        def load_q1(i):
             q1_sb[i] = xin.tile([P, C * G], BF16, name="q1_sb")
             nc.sync.dma_start(out=q1_sb[i][:], in_=q1_t[i])
 
-        def tx_x(i):
-            grp[i] = work.tile([P, NPOS, P, PACK], BF16, align_bytes=64, name="grp")
-            codes[i] = work.tile([P, NPOS, P], U32, align_bytes=64, name="codes")
-            scales[i] = work.tile([P, NPOS, P], U8, align_bytes=64, name="scales")
-            xw = x_sb[i][:].bitcast(F32).rearrange("p (i t g) -> p t g i", t=PACK, g=G)
-            banks = []
-            for g in range(G):
-                xt = pst.tile([P, PACK * P], F32, tag="tr", name="xt")
-                for t in range(PACK):
-                    nc.tensor.transpose(xt[:, t * P:(t + 1) * P], xw[:, t, g, :], ident_f[:])
-                banks.append(xt)
-            return banks
+        def x_words(i):
+            return x_sb[i][:].bitcast(F32).rearrange("p (i t g) -> p t i g", t=PACK, g=G)
 
-        def ev_x(i, g, xt):
-            nc.scalar.copy(
+        def separate_x(i):
+            xs[i] = sep.tile([P, G - RAW, PACK, P], F32, name="xs")
+            nc.scalar.copy(out=xs[i][:].rearrange("p g t i -> p t i g"), in_=x_words(i)[:, :, :, RAW:G])
+
+        def separate(engine_copy, rows, name):
+            dst = sep.tile([P, 3, 2, P, 2], BF16, name=name)
+            for u in range(2):
+                engine_copy(
+                    out=dst[:, :, u, :, :].rearrange("p s i e -> p i e s"),
+                    in_=rows.rearrange("p (i u e s) -> p u i e s", u=2, e=2, s=3)[:, u, :, :, :],
+                )
+            return dst
+
+        def tx_x(i, g):
+            xt = pst.tile([P, PACK, P], F32, tag="tr", name="xt")
+            for t in range(PACK):
+                src = x_words(i)[:, t, :, g] if g < RAW else xs[i][:, g - RAW, t, :]
+                nc.tensor.transpose(xt[:, t, :], src, ident_f[:])
+            return xt
+
+        def ev_x(engine_copy, i, g, xt):
+            engine_copy(
                 out=grp[i][:, 2 * g:2 * g + 2, :, :],
-                in_=xt[:].bitcast(BF16).rearrange("p (t m k) -> p k m t", t=PACK, k=2),
+                in_=xt[:].rearrange("p t m -> p (t m)").bitcast(BF16).rearrange("p (t m k) -> p k m t", t=PACK, k=2),
             )
 
-        def tx_triples(rows, a):
-            words = rows.bitcast(F32).rearrange("p (i a r) -> p a r i", a=2, r=3)
-            bank = pst.tile([P, PACK * P], F32, tag="tr", name="bank")
-            for r in range(3):
-                nc.tensor.transpose(bank[:, r * P:(r + 1) * P], words[:, a, r, :], ident_f[:])
+        def tx_triples(src, s0, s1):
+            words = src[:].rearrange("p s u i e -> p (s u i e)").bitcast(F32).rearrange("p (s u i) -> p s u i", s=3, u=2)
+            bank = pst.tile([P, s1 - s0, 2, P], F32, tag="tr", name="bank")
+            for s in range(s0, s1):
+                for u in range(2):
+                    nc.tensor.transpose(bank[:, s - s0, u, :], words[:, s, u, :], ident_f[:])
             return bank
 
-        def pick(bank, s):
-            off = [256 * ((3 * e + s) // 2) + (3 * e + s) % 2 for e in range(2)]
-            step = off[1] - off[0]
-            flat = bank[:].bitcast(BF16)[:, off[0]:off[0] + 2 * step]
-            cols = flat.rearrange("p (e b) -> p e b", e=2)[:, :, 0:2 * P]
-            return cols.rearrange("p e (j s) -> p j e s", s=2)[:, :, :, 0]
+        def ev_triples(engine_copy, dst, bank):
+            engine_copy(out=dst, in_=bank[:].rearrange("p s u j -> p s j u"))
 
-        def ev_q(i, a, bank):
-            for g in range(G):
-                nc.vector.tensor_copy(out=grp[i][:, 6 + g, :, 2 * a:2 * a + 2], in_=pick(bank, g))
+        def grp_words(tile):
+            return tile[:].rearrange("p a m u -> p (a m u)").bitcast(F32).rearrange("p (a m u) -> p a m u", a=tile.shape[1], u=2)
 
         def quant(i, p0, npos):
             nc.vector.quantize_mx(
@@ -97,19 +101,16 @@ def tile_quadjetresnetblock_pb_t_kernel(tc, x, q2, q1, W3, b3, out):
                 in_=grp[i][:, p0:p0 + npos, :, :].rearrange("p a m u -> p (a m u)"),
             )
 
-        def residual_part(engine, i, oc):
-            cols = slice(oc * P * G, (oc + 1) * P * G)
-            engine.tensor_tensor(
-                out=acc[i][:, cols].rearrange("p (o g) -> p o g", g=G),
-                in0=q1_sb[i][:, cols].rearrange("p (o g) -> p o g", g=G),
-                in1=b_bc[:, oc * P:(oc + 1) * P].unsqueeze(2).to_broadcast([P, P, G]),
-                op=ADD,
-            )
-
         def residual(i):
             acc[i] = res.tile([P, O * G], F32, name="acc")
             for oc in range(OT):
-                residual_part(nc.gpsimd if oc < OC_POOL else nc.vector, i, oc)
+                cols = slice(oc * P * G, (oc + 1) * P * G)
+                nc.gpsimd.tensor_tensor(
+                    out=acc[i][:, cols].rearrange("p (o g) -> p o g", g=G),
+                    in0=q1_sb[i][:, cols].rearrange("p (o g) -> p o g", g=G),
+                    in1=b_bc[:, oc * P:(oc + 1) * P].unsqueeze(2).to_broadcast([P, P, G]),
+                    op=ADD,
+                )
 
         def mm(i, oc):
             ps[oc] = psm.tile([P, G, P], F32, tag="mm", name="ps")
@@ -134,85 +135,75 @@ def tile_quadjetresnetblock_pb_t_kernel(tc, x, q2, q1, W3, b3, out):
             lo, hi = oc0 * P * G, oc1 * P * G
             part = acc[i][:, lo:hi]
             nc.scalar.activation(out=part, in_=part, func=RELU)
-            nc.scalar.dma_start(out=out_t[i][:, lo:hi], in_=part)
-
-        def prepare(i):
-            xb = tx_x(i)
-            for g in range(G):
-                ev_x(i, g, xb[g])
-            quant(i, 0, 4)
-            for a in range(2):
-                ev_q(i, a, tx_triples(q2_sb[i][:], a))
-            quant(i, 4, 4)
-            quant(i, 8, 1)
+            nc.sync.dma_start(out=out_t[i][:, lo:hi], in_=part)
 
         w_sb = const.tile([P, 4, C * KW], BF16)
         for d in range(4):
             nc.sync.dma_start(out=w_sb[:, d, :], in_=w_t[d])
         b_bc = const.tile([P, O], BF16)
         nc.scalar.dma_start(out=b_bc[:], in_=b3.partition_broadcast(P))
-        for i in range(LAG):
-            load_xq(i)
-        for i in range(LAG):
-            load_q1(i)
-        for i in range(LAG, AHEAD):
-            load_xq(i)
-            load_q1(i)
+        for i in range(AHEAD):
+            load(i)
         ident_f = const.tile([P, P], F32)
         make_identity(nc, ident_f[:])
 
         w_grp = const.tile([P, KW, O, PACK], BF16, align_bytes=64)
         w_codes = const.tile([P, KW, O], U32, align_bytes=64)
         w_scales = const.tile([P, KW, O], U8, align_bytes=64)
+        copies = (nc.vector.tensor_copy, nc.scalar.copy)
         for d in range(4):
-            for a in range(2):
-                bank = tx_triples(w_sb[:, d, :], a)
-                for k in range(KW):
-                    dst = w_grp[:, k, d * P:(d + 1) * P, 2 * a:2 * a + 2]
-                    if a == 0:
-                        nc.vector.tensor_copy(out=dst, in_=pick(bank, k))
-                    else:
-                        nc.scalar.copy(out=dst, in_=pick(bank, k))
+            ws = separate(copies[d % 2], w_sb[:, d, :], "ws")
+            for s0, s1 in ((0, 2), (2, 3)):
+                ev_triples(copies[d % 2], grp_words(w_grp)[:, s0:s1, d * P:(d + 1) * P, :], tx_triples(ws, s0, s1))
         for k in range(KW):
             nc.vector.quantize_mx(
                 out=w_codes[:, k, :].bitcast(FP8X4),
                 scales=w_scales[:, k, :],
                 in_=w_grp[:, k, :, :].rearrange("p o u -> p (o u)"),
             )
-        for i in range(LAG):
-            prepare(i)
-            residual(i)
 
-        for i in range(NT):
-            nxt = i + LAG
-            more = nxt < NT
-            if i + AHEAD < NT:
-                load_xq(i + AHEAD)
-                load_q1(i + AHEAD)
-            if more:
-                residual(nxt)
-                xb = tx_x(nxt)
-                for g in range(G):
-                    ev_x(nxt, g, xb[g])
+        for i in range(-3, NT):
+            a, t, q = i + 3, i + 2, i + 1
+            if i >= 0 and i + AHEAD < NT:
+                load(i + AHEAD)
+            if a < NT:
+                separate_x(a)
+                qs[a] = separate(nc.vector.tensor_copy, q2_sb[a][:], "qs")
             if i > 0:
-                add(i - 1, 2)
                 add(i - 1, 3)
+            if 0 <= q < NT:
+                residual(q)
+            if 0 <= t < NT:
+                grp[t] = work.tile([P, NPOS, P, PACK], BF16, align_bytes=64, name="grp")
+                gw = grp_words(grp[t])
+                xt = [tx_x(t, g) for g in range(G)]
+                q01 = tx_triples(qs[t], 0, 2)
+                q2b = tx_triples(qs[t], 2, 3)
+                ev_x(nc.vector.tensor_copy, t, 0, xt[0])
+                ev_x(nc.scalar.copy, t, 1, xt[1])
+                ev_x(nc.scalar.copy, t, 2, xt[2])
+                ev_triples(nc.vector.tensor_copy, gw[:, 6:8, :, :], q01)
+                ev_triples(nc.scalar.copy, gw[:, 8:9, :, :], q2b)
+            if i > 0:
                 relu_store(i - 1, 0, OT)
-            mm(i, 0)
-            mm(i, 1)
-            add(i, 0)
-            if more:
-                quant(nxt, 0, 4)
-            add(i, 1)
-            if more:
-                for a in range(2):
-                    ev_q(nxt, a, tx_triples(q2_sb[nxt][:], a))
-                quant(nxt, 4, 4)
-                quant(nxt, 8, 1)
-            mm(i, 2)
-            mm(i, 3)
-        relu_store(NT - 1, 0, 2)
-        add(NT - 1, 2)
-        relu_store(NT - 1, 2, 3)
+            if 0 <= q < NT:
+                codes[q] = work.tile([P, NPOS, P], U32, align_bytes=64, name="codes")
+                scales[q] = work.tile([P, NPOS, P], U8, align_bytes=64, name="scales")
+                quant(q, 0, 4)
+            if i >= 0:
+                mm(i, 0)
+                add(i, 0)
+            if 0 <= q < NT:
+                quant(q, 4, 4)
+            if i >= 0:
+                mm(i, 1)
+                add(i, 1)
+            if 0 <= q < NT:
+                quant(q, 8, 1)
+            if i >= 0:
+                mm(i, 2)
+                add(i, 2)
+                mm(i, 3)
+        relu_store(NT - 1, 0, 3)
         add(NT - 1, 3)
         relu_store(NT - 1, 3, 4)

@@ -37,8 +37,8 @@ def tile_quadjetresnetblock_pb_t_kernel(tc, x, q2, q1, W3, b3, out):
         sep = ctx.enter_context(tc.tile_pool(name="sep", bufs=2))
         work = ctx.enter_context(tc.tile_pool(name="work", bufs=2))
         res = ctx.enter_context(tc.tile_pool(name="res", bufs=4))
-        pst = ctx.enter_context(tc.psum_pool(name="pst", bufs=5))
-        psm = ctx.enter_context(tc.psum_pool(name="psm", bufs=3))
+        pst = ctx.enter_context(tc.psum_pool(name="pst", bufs=4))
+        psm = ctx.enter_context(tc.psum_pool(name="psm", bufs=4))
         ctx.enter_context(tc.manual_schedule())
 
         x_sb, q2_sb, q1_sb, xs, qs, grp, codes, scales, acc, ps = {}, {}, {}, {}, {}, {}, {}, {}, {}, {}
@@ -103,6 +103,7 @@ def tile_quadjetresnetblock_pb_t_kernel(tc, x, q2, q1, W3, b3, out):
 
         def residual(i):
             acc[i] = res.tile([P, O * G], F32, name="acc")
+            nc.vector.memset(acc[i][:, 0:1], 0.0)
             for oc in range(OT):
                 cols = slice(oc * P * G, (oc + 1) * P * G)
                 nc.gpsimd.tensor_tensor(
@@ -166,44 +167,31 @@ def tile_quadjetresnetblock_pb_t_kernel(tc, x, q2, q1, W3, b3, out):
             a, t, q = i + 3, i + 2, i + 1
             if i >= 0 and i + AHEAD < NT:
                 load(i + AHEAD)
-            if a < NT:
-                separate_x(a)
-                qs[a] = separate(nc.vector.tensor_copy, q2_sb[a][:], "qs")
-            if i > 0:
-                add(i - 1, 3)
-            if 0 <= q < NT:
-                residual(q)
-            if 0 <= t < NT:
-                grp[t] = work.tile([P, NPOS, P, PACK], BF16, align_bytes=64, name="grp")
-                gw = grp_words(grp[t])
-                xt = [tx_x(t, g) for g in range(G)]
-                q01 = tx_triples(qs[t], 0, 2)
-                q2b = tx_triples(qs[t], 2, 3)
-                ev_x(nc.vector.tensor_copy, t, 0, xt[0])
-                ev_x(nc.scalar.copy, t, 1, xt[1])
-                ev_x(nc.scalar.copy, t, 2, xt[2])
-                ev_triples(nc.vector.tensor_copy, gw[:, 6:8, :, :], q01)
-                ev_triples(nc.scalar.copy, gw[:, 8:9, :, :], q2b)
-            if i > 0:
-                relu_store(i - 1, 0, OT)
-            if 0 <= q < NT:
+            mult, quantize, turn = i >= 0, 0 <= q < NT, 0 <= t < NT
+            if quantize:
                 codes[q] = work.tile([P, NPOS, P], U32, align_bytes=64, name="codes")
                 scales[q] = work.tile([P, NPOS, P], U8, align_bytes=64, name="scales")
                 quant(q, 0, 4)
-            if i >= 0:
-                mm(i, 0)
-                add(i, 0)
-            if 0 <= q < NT:
                 quant(q, 4, 4)
-            if i >= 0:
-                mm(i, 1)
-                add(i, 1)
-            if 0 <= q < NT:
                 quant(q, 8, 1)
-            if i >= 0:
-                mm(i, 2)
-                add(i, 2)
-                mm(i, 3)
-        relu_store(NT - 1, 0, 3)
-        add(NT - 1, 3)
-        relu_store(NT - 1, 3, 4)
+            if a < NT:
+                separate_x(a)
+                qs[a] = separate(nc.vector.tensor_copy, q2_sb[a][:], "qs")
+            if quantize:
+                residual(q)
+            if i > 0:
+                relu_store(i - 1, 0, OT)
+            if mult:
+                for oc in range(OT):
+                    mm(i, oc)
+                    add(i, oc)
+            if turn:
+                grp[t] = work.tile([P, NPOS, P, PACK], BF16, align_bytes=64, name="grp")
+                gw = grp_words(grp[t])
+                ev_x(nc.scalar.copy, t, 1, tx_x(t, 1))
+                ev_x(nc.vector.tensor_copy, t, 0, tx_x(t, 0))
+                ev_x(nc.scalar.copy, t, 2, tx_x(t, 2))
+                ev_triples(nc.vector.tensor_copy, gw[:, 6:8, :, :], tx_triples(qs[t], 0, 2))
+                ev_triples(nc.scalar.copy, gw[:, 8:9, :, :], tx_triples(qs[t], 2, 3))
+        for oc0, oc1 in ((0, 2), (2, 3), (3, 4)):
+            relu_store(NT - 1, oc0, oc1)

@@ -18,7 +18,7 @@ NT = N // P
 PACK = 4
 OT = O // P
 NPOS = 9
-RAW = 1
+OC_POOL = 3
 AHEAD = 5
 FLOPS = 2 * N * G * O * C * KW
 
@@ -41,7 +41,7 @@ def tile_quadjetresnetblock_pb_t_kernel(tc, x, q2, q1, W3, b3, out):
         psm = ctx.enter_context(tc.psum_pool(name="psm", bufs=4))
         ctx.enter_context(tc.manual_schedule())
 
-        x_sb, q2_sb, q1_sb, xs, qs, grp, codes, scales, acc, ps = {}, {}, {}, {}, {}, {}, {}, {}, {}, {}
+        x_sb, q2_sb, q1_sb, qs, grp, codes, scales, acc, ps = {}, {}, {}, {}, {}, {}, {}, {}, {}
 
         def load(i):
             x_sb[i] = xin.tile([P, C * 6], BF16, name="x_sb")
@@ -53,10 +53,6 @@ def tile_quadjetresnetblock_pb_t_kernel(tc, x, q2, q1, W3, b3, out):
 
         def x_words(i):
             return x_sb[i][:].bitcast(F32).rearrange("p (i t g) -> p t i g", t=PACK, g=G)
-
-        def separate_x(i):
-            xs[i] = sep.tile([P, G - RAW, PACK, P], F32, name="xs")
-            nc.scalar.copy(out=xs[i][:].rearrange("p g t i -> p t i g"), in_=x_words(i)[:, :, :, RAW:G])
 
         def separate(engine_copy, rows, name):
             dst = sep.tile([P, 3, 2, P, 2], BF16, name=name)
@@ -70,8 +66,7 @@ def tile_quadjetresnetblock_pb_t_kernel(tc, x, q2, q1, W3, b3, out):
         def tx_x(i, g):
             xt = pst.tile([P, PACK, P], F32, tag="tr", name="xt")
             for t in range(PACK):
-                src = x_words(i)[:, t, :, g] if g < RAW else xs[i][:, g - RAW, t, :]
-                nc.tensor.transpose(xt[:, t, :], src, ident_f[:])
+                nc.tensor.transpose(xt[:, t, :], x_words(i)[:, t, :, g], ident_f[:])
             return xt
 
         def ev_x(engine_copy, i, g, xt):
@@ -101,17 +96,22 @@ def tile_quadjetresnetblock_pb_t_kernel(tc, x, q2, q1, W3, b3, out):
                 in_=grp[i][:, p0:p0 + npos, :, :].rearrange("p a m u -> p (a m u)"),
             )
 
+        def residual_part(engine, i, oc):
+            cols = slice(oc * P * G, (oc + 1) * P * G)
+            engine.tensor_tensor(
+                out=acc[i][:, cols].rearrange("p (o g) -> p o g", g=G),
+                in0=q1_sb[i][:, cols].rearrange("p (o g) -> p o g", g=G),
+                in1=b_bc[:, oc * P:(oc + 1) * P].unsqueeze(2).to_broadcast([P, P, G]),
+                op=ADD,
+            )
+
         def residual(i):
             acc[i] = res.tile([P, O * G], F32, name="acc")
+            for oc in range(OC_POOL, OT):
+                residual_part(nc.vector, i, oc)
             nc.vector.memset(acc[i][:, 0:1], 0.0)
-            for oc in range(OT):
-                cols = slice(oc * P * G, (oc + 1) * P * G)
-                nc.gpsimd.tensor_tensor(
-                    out=acc[i][:, cols].rearrange("p (o g) -> p o g", g=G),
-                    in0=q1_sb[i][:, cols].rearrange("p (o g) -> p o g", g=G),
-                    in1=b_bc[:, oc * P:(oc + 1) * P].unsqueeze(2).to_broadcast([P, P, G]),
-                    op=ADD,
-                )
+            for oc in range(OC_POOL):
+                residual_part(nc.gpsimd, i, oc)
 
         def mm(i, oc):
             ps[oc] = psm.tile([P, G, P], F32, tag="mm", name="ps")
@@ -151,11 +151,10 @@ def tile_quadjetresnetblock_pb_t_kernel(tc, x, q2, q1, W3, b3, out):
         w_grp = const.tile([P, KW, O, PACK], BF16, align_bytes=64)
         w_codes = const.tile([P, KW, O], U32, align_bytes=64)
         w_scales = const.tile([P, KW, O], U8, align_bytes=64)
-        copies = (nc.vector.tensor_copy, nc.scalar.copy)
         for d in range(4):
-            ws = separate(copies[d % 2], w_sb[:, d, :], "ws")
+            ws = separate(nc.vector.tensor_copy, w_sb[:, d, :], "ws")
             for s0, s1 in ((0, 2), (2, 3)):
-                ev_triples(copies[d % 2], grp_words(w_grp)[:, s0:s1, d * P:(d + 1) * P, :], tx_triples(ws, s0, s1))
+                ev_triples(nc.scalar.copy, grp_words(w_grp)[:, s0:s1, d * P:(d + 1) * P, :], tx_triples(ws, s0, s1))
         for k in range(KW):
             nc.vector.quantize_mx(
                 out=w_codes[:, k, :].bitcast(FP8X4),
@@ -168,19 +167,15 @@ def tile_quadjetresnetblock_pb_t_kernel(tc, x, q2, q1, W3, b3, out):
             if i >= 0 and i + AHEAD < NT:
                 load(i + AHEAD)
             mult, quantize, turn = i >= 0, 0 <= q < NT, 0 <= t < NT
+            if a < NT:
+                qs[a] = separate(nc.vector.tensor_copy, q2_sb[a][:], "qs")
             if quantize:
                 codes[q] = work.tile([P, NPOS, P], U32, align_bytes=64, name="codes")
                 scales[q] = work.tile([P, NPOS, P], U8, align_bytes=64, name="scales")
                 quant(q, 0, 4)
                 quant(q, 4, 4)
                 quant(q, 8, 1)
-            if a < NT:
-                separate_x(a)
-                qs[a] = separate(nc.vector.tensor_copy, q2_sb[a][:], "qs")
-            if quantize:
                 residual(q)
-            if i > 0:
-                relu_store(i - 1, 0, OT)
             if mult:
                 for oc in range(OT):
                     mm(i, oc)
@@ -188,10 +183,11 @@ def tile_quadjetresnetblock_pb_t_kernel(tc, x, q2, q1, W3, b3, out):
             if turn:
                 grp[t] = work.tile([P, NPOS, P, PACK], BF16, align_bytes=64, name="grp")
                 gw = grp_words(grp[t])
-                ev_x(nc.scalar.copy, t, 1, tx_x(t, 1))
-                ev_x(nc.vector.tensor_copy, t, 0, tx_x(t, 0))
-                ev_x(nc.scalar.copy, t, 2, tx_x(t, 2))
+                for g in range(G):
+                    ev_x(nc.scalar.copy, t, g, tx_x(t, g))
                 ev_triples(nc.vector.tensor_copy, gw[:, 6:8, :, :], tx_triples(qs[t], 0, 2))
                 ev_triples(nc.scalar.copy, gw[:, 8:9, :, :], tx_triples(qs[t], 2, 3))
+            if i > 0:
+                relu_store(i - 1, 0, OT)
         for oc0, oc1 in ((0, 2), (2, 3), (3, 4)):
             relu_store(NT - 1, oc0, oc1)

@@ -18,7 +18,7 @@ NT = N // P
 PACK = 4
 OT = O // P
 NPOS = 9
-OC_POOL = 3
+OC_POOL = 2
 AHEAD = 5
 FLOPS = 2 * N * G * O * C * KW
 
@@ -141,8 +141,11 @@ def tile_quadjetresnetblock_pb_t_kernel(tc, x, q2, q1, W3, b3, out):
         w_sb = const.tile([P, 4, C * KW], BF16)
         for d in range(4):
             nc.sync.dma_start(out=w_sb[:, d, :], in_=w_t[d])
-        b_bc = const.tile([P, O], BF16)
-        nc.scalar.dma_start(out=b_bc[:], in_=b3.partition_broadcast(P))
+        b_row = const.tile([P, O], BF16)
+        nc.gpsimd.memset(b_row[:], 0.0)
+        nc.scalar.dma_start(out=b_row[0:1, :], in_=b3.unsqueeze(0))
+        ones = const.tile([P, P], BF16)
+        nc.gpsimd.memset(ones[:], 1.0)
         for i in range(AHEAD):
             load(i)
         ident_f = const.tile([P, P], F32)
@@ -161,6 +164,11 @@ def tile_quadjetresnetblock_pb_t_kernel(tc, x, q2, q1, W3, b3, out):
                 scales=w_scales[:, k, :],
                 in_=w_grp[:, k, :, :].rearrange("p o u -> p (o u)"),
             )
+
+        b_ps = pst.tile([P, O], F32, tag="tr", name="b_ps")
+        nc.tensor.matmul(b_ps[:], ones[:], b_row[:], start=True, stop=True)
+        b_bc = const.tile([P, O], BF16)
+        nc.scalar.copy(out=b_bc[:], in_=b_ps[:])
 
         for i in range(-3, NT):
             a, t, q = i + 3, i + 2, i + 1
@@ -185,7 +193,7 @@ def tile_quadjetresnetblock_pb_t_kernel(tc, x, q2, q1, W3, b3, out):
                 gw = grp_words(grp[t])
                 for g in range(G):
                     ev_x(nc.scalar.copy, t, g, tx_x(t, g))
-                ev_triples(nc.vector.tensor_copy, gw[:, 6:8, :, :], tx_triples(qs[t], 0, 2))
+                ev_triples(nc.scalar.copy, gw[:, 6:8, :, :], tx_triples(qs[t], 0, 2))
                 ev_triples(nc.scalar.copy, gw[:, 8:9, :, :], tx_triples(qs[t], 2, 3))
             if i > 0:
                 relu_store(i - 1, 0, OT)

@@ -18,7 +18,7 @@ NT = N // P
 PACK = 4
 OT = O // P
 NPOS = 9
-OC_POOL = 2
+O_POOL = 256
 AHEAD = 5
 FLOPS = 2 * N * G * O * C * KW
 
@@ -34,14 +34,14 @@ def tile_quadjetresnetblock_pb_t_kernel(tc, x, q2, q1, W3, b3, out):
     with ExitStack() as ctx:
         const = ctx.enter_context(tc.tile_pool(name="const", bufs=1))
         xin = ctx.enter_context(tc.tile_pool(name="xin", bufs=AHEAD + 1))
-        sep = ctx.enter_context(tc.tile_pool(name="sep", bufs=2))
-        work = ctx.enter_context(tc.tile_pool(name="work", bufs=2))
+        sep = ctx.enter_context(tc.tile_pool(name="sep", bufs=3))
+        work = ctx.enter_context(tc.tile_pool(name="work", bufs=3))
         res = ctx.enter_context(tc.tile_pool(name="res", bufs=4))
         pst = ctx.enter_context(tc.psum_pool(name="pst", bufs=4))
         psm = ctx.enter_context(tc.psum_pool(name="psm", bufs=4))
         ctx.enter_context(tc.manual_schedule())
 
-        x_sb, q2_sb, q1_sb, qs, grp, codes, scales, acc, ps = {}, {}, {}, {}, {}, {}, {}, {}, {}
+        x_sb, q2_sb, q1_sb, xs, qs, grp, codes, scales, acc, ps = {}, {}, {}, {}, {}, {}, {}, {}, {}, {}
 
         def load(i):
             x_sb[i] = xin.tile([P, C * 6], BF16, name="x_sb")
@@ -53,6 +53,10 @@ def tile_quadjetresnetblock_pb_t_kernel(tc, x, q2, q1, W3, b3, out):
 
         def x_words(i):
             return x_sb[i][:].bitcast(F32).rearrange("p (i t g) -> p t i g", t=PACK, g=G)
+
+        def separate_x(i):
+            xs[i] = sep.tile([P, 1, PACK, P], F32, name="xs")
+            nc.vector.tensor_copy(out=xs[i][:, 0, :, :].rearrange("p t i -> p i t"), in_=x_words(i)[:, :, :, 2].rearrange("p t i -> p i t"))
 
         def separate(engine_copy, rows, name):
             dst = sep.tile([P, 3, 2, P, 2], BF16, name=name)
@@ -66,7 +70,8 @@ def tile_quadjetresnetblock_pb_t_kernel(tc, x, q2, q1, W3, b3, out):
         def tx_x(i, g):
             xt = pst.tile([P, PACK, P], F32, tag="tr", name="xt")
             for t in range(PACK):
-                nc.tensor.transpose(xt[:, t, :], x_words(i)[:, t, :, g], ident_f[:])
+                src = (x_words(i)[:, t, :, 0], x_words(i)[:, t, :, 1], xs[i][:, 0, t, :])[g]
+                nc.tensor.transpose(xt[:, t, :], src, ident_f[:])
             return xt
 
         def ev_x(engine_copy, i, g, xt):
@@ -96,22 +101,20 @@ def tile_quadjetresnetblock_pb_t_kernel(tc, x, q2, q1, W3, b3, out):
                 in_=grp[i][:, p0:p0 + npos, :, :].rearrange("p a m u -> p (a m u)"),
             )
 
-        def residual_part(engine, i, oc):
-            cols = slice(oc * P * G, (oc + 1) * P * G)
+        def residual_part(engine, i, o0, o1):
+            part = slice(o0 * G, o1 * G)
             engine.tensor_tensor(
-                out=acc[i][:, cols].rearrange("p (o g) -> p o g", g=G),
-                in0=q1_sb[i][:, cols].rearrange("p (o g) -> p o g", g=G),
-                in1=b_bc[:, oc * P:(oc + 1) * P].unsqueeze(2).to_broadcast([P, P, G]),
+                out=acc[i][:, part].rearrange("p (o g) -> p o g", g=G),
+                in0=q1_sb[i][:, part].rearrange("p (o g) -> p o g", g=G),
+                in1=b_bc[:, o0:o1].unsqueeze(2).to_broadcast([P, o1 - o0, G]),
                 op=ADD,
             )
 
         def residual(i):
             acc[i] = res.tile([P, O * G], F32, name="acc")
-            for oc in range(OC_POOL, OT):
-                residual_part(nc.vector, i, oc)
+            residual_part(nc.vector, i, O_POOL, O)
             nc.vector.memset(acc[i][:, 0:1], 0.0)
-            for oc in range(OC_POOL):
-                residual_part(nc.gpsimd, i, oc)
+            residual_part(nc.gpsimd, i, 0, O_POOL)
 
         def mm(i, oc):
             ps[oc] = psm.tile([P, G, P], F32, tag="mm", name="ps")
@@ -138,63 +141,93 @@ def tile_quadjetresnetblock_pb_t_kernel(tc, x, q2, q1, W3, b3, out):
             nc.scalar.activation(out=part, in_=part, func=RELU)
             nc.sync.dma_start(out=out_t[i][:, lo:hi], in_=part)
 
+        def separate_rows(i):
+            qs[i] = separate(nc.vector.tensor_copy, q2_sb[i][:], "qs")
+            separate_x(i)
+
+        def turn(i):
+            grp[i] = work.tile([P, NPOS, P, PACK], BF16, align_bytes=64, name="grp")
+            gw = grp_words(grp[i])
+            ev_x(nc.scalar.copy, i, 0, tx_x(i, 0))
+            ev_x(nc.scalar.copy, i, 1, tx_x(i, 1))
+            ev_x(nc.scalar.copy, i, 2, tx_x(i, 2))
+            ev_triples(nc.scalar.copy, gw[:, 6:8, :, :], tx_triples(qs[i], 0, 2))
+            ev_triples(nc.scalar.copy, gw[:, 8:9, :, :], tx_triples(qs[i], 2, 3))
+
+        def turn_first(i):
+            grp[i] = work.tile([P, NPOS, P, PACK], BF16, align_bytes=64, name="grp")
+            gw = grp_words(grp[i])
+            ev_x(nc.scalar.copy, i, 0, tx_x(i, 0))
+            ev_x(nc.scalar.copy, i, 1, tx_x(i, 1))
+            ev_x(nc.scalar.copy, i, 2, tx_x(i, 2))
+            ev_triples(nc.scalar.copy, gw[:, 6:8, :, :], tx_triples(qs[i], 0, 2))
+            ev_triples(nc.scalar.copy, gw[:, 8:9, :, :], tx_triples(qs[i], 2, 3))
+
+        def open_codes(i):
+            codes[i] = work.tile([P, NPOS, P], U32, align_bytes=64, name="codes")
+            scales[i] = work.tile([P, NPOS, P], U8, align_bytes=64, name="scales")
+
+        def multiply(i):
+            for oc in range(OT):
+                mm(i, oc)
+                add(i, oc)
+
         w_sb = const.tile([P, 4, C * KW], BF16)
+        b_row = const.tile([P, O], BF16)
+        nc.vector.memset(b_row[:], 0.0)
         for d in range(4):
             nc.sync.dma_start(out=w_sb[:, d, :], in_=w_t[d])
-        b_row = const.tile([P, O], BF16)
-        nc.gpsimd.memset(b_row[:], 0.0)
-        nc.scalar.dma_start(out=b_row[0:1, :], in_=b3.unsqueeze(0))
-        ones = const.tile([P, P], BF16)
-        nc.gpsimd.memset(ones[:], 1.0)
+        nc.sync.dma_start(out=b_row[0:1, :], in_=b3.unsqueeze(0))
         for i in range(AHEAD):
             load(i)
         ident_f = const.tile([P, P], F32)
         make_identity(nc, ident_f[:])
+        ones = const.tile([P, P], BF16)
+        nc.gpsimd.memset(ones[:], 1.0)
 
         w_grp = const.tile([P, KW, O, PACK], BF16, align_bytes=64)
         w_codes = const.tile([P, KW, O], U32, align_bytes=64)
         w_scales = const.tile([P, KW, O], U8, align_bytes=64)
         for d in range(4):
-            ws = separate(nc.vector.tensor_copy, w_sb[:, d, :], "ws")
+            ws = separate((nc.vector.tensor_copy, nc.vector.tensor_copy, nc.vector.tensor_copy, nc.vector.tensor_copy)[d], w_sb[:, d, :], "ws")
             for s0, s1 in ((0, 2), (2, 3)):
-                ev_triples(nc.scalar.copy, grp_words(w_grp)[:, s0:s1, d * P:(d + 1) * P, :], tx_triples(ws, s0, s1))
+                ev_triples((nc.scalar.copy, nc.scalar.copy, nc.scalar.copy, nc.scalar.copy)[d], grp_words(w_grp)[:, s0:s1, d * P:(d + 1) * P, :], tx_triples(ws, s0, s1))
+        separate_rows(0)
+        turn_first(0)
         for k in range(KW):
             nc.vector.quantize_mx(
                 out=w_codes[:, k, :].bitcast(FP8X4),
                 scales=w_scales[:, k, :],
                 in_=w_grp[:, k, :, :].rearrange("p o u -> p (o u)"),
             )
-
         b_ps = pst.tile([P, O], F32, tag="tr", name="b_ps")
         nc.tensor.matmul(b_ps[:], ones[:], b_row[:], start=True, stop=True)
         b_bc = const.tile([P, O], BF16)
         nc.scalar.copy(out=b_bc[:], in_=b_ps[:])
+        open_codes(0)
+        quant(0, 0, 4)
+        separate_rows(1)
+        quant(0, 4, 4)
+        quant(0, 8, 1)
+        residual(0)
+        turn(1)
+        separate_rows(2)
 
-        for i in range(-3, NT):
-            a, t, q = i + 3, i + 2, i + 1
-            if i >= 0 and i + AHEAD < NT:
+        for i in range(NT):
+            if i + AHEAD < NT:
                 load(i + AHEAD)
-            mult, quantize, turn = i >= 0, 0 <= q < NT, 0 <= t < NT
-            if a < NT:
-                qs[a] = separate(nc.vector.tensor_copy, q2_sb[a][:], "qs")
-            if quantize:
-                codes[q] = work.tile([P, NPOS, P], U32, align_bytes=64, name="codes")
-                scales[q] = work.tile([P, NPOS, P], U8, align_bytes=64, name="scales")
-                quant(q, 0, 4)
-                quant(q, 4, 4)
-                quant(q, 8, 1)
-                residual(q)
-            if mult:
-                for oc in range(OT):
-                    mm(i, oc)
-                    add(i, oc)
-            if turn:
-                grp[t] = work.tile([P, NPOS, P, PACK], BF16, align_bytes=64, name="grp")
-                gw = grp_words(grp[t])
-                for g in range(G):
-                    ev_x(nc.scalar.copy, t, g, tx_x(t, g))
-                ev_triples(nc.scalar.copy, gw[:, 6:8, :, :], tx_triples(qs[t], 0, 2))
-                ev_triples(nc.scalar.copy, gw[:, 8:9, :, :], tx_triples(qs[t], 2, 3))
+            if i + 1 < NT:
+                open_codes(i + 1)
+                quant(i + 1, 0, 4)
+            if i + 3 < NT:
+                separate_rows(i + 3)
+            if i + 1 < NT:
+                quant(i + 1, 4, 4)
+                quant(i + 1, 8, 1)
+                residual(i + 1)
+            if i + 2 < NT:
+                turn(i + 2)
+            multiply(i)
             if i > 0:
                 relu_store(i - 1, 0, OT)
         for oc0, oc1 in ((0, 2), (2, 3), (3, 4)):

@@ -9,6 +9,7 @@ U32 = mybir.dt.uint32
 U8 = mybir.dt.uint8
 FP8X4 = mybir.dt.float8_e4m3fn_x4
 ADD = mybir.AluOpType.add
+MAX = mybir.AluOpType.max
 RELU = mybir.ActivationFunctionType.Relu
 
 P = 128
@@ -18,8 +19,9 @@ NT = N // P
 PACK = 4
 OT = O // P
 NPOS = 9
-O_POOL = 256
+O_POOL = 320
 AHEAD = 5
+O_RELU = 448
 FLOPS = 2 * N * G * O * C * KW
 
 
@@ -37,8 +39,8 @@ def tile_quadjetresnetblock_pb_t_kernel(tc, x, q2, q1, W3, b3, out):
         sep = ctx.enter_context(tc.tile_pool(name="sep", bufs=3))
         work = ctx.enter_context(tc.tile_pool(name="work", bufs=3))
         res = ctx.enter_context(tc.tile_pool(name="res", bufs=4))
-        pst = ctx.enter_context(tc.psum_pool(name="pst", bufs=4))
-        psm = ctx.enter_context(tc.psum_pool(name="psm", bufs=4))
+        pst = ctx.enter_context(tc.psum_pool(name="pst", bufs=5))
+        psm = ctx.enter_context(tc.psum_pool(name="psm", bufs=3))
         ctx.enter_context(tc.manual_schedule())
 
         x_sb, q2_sb, q1_sb, xs, qs, grp, codes, scales, acc, ps = {}, {}, {}, {}, {}, {}, {}, {}, {}, {}
@@ -54,10 +56,6 @@ def tile_quadjetresnetblock_pb_t_kernel(tc, x, q2, q1, W3, b3, out):
         def x_words(i):
             return x_sb[i][:].bitcast(F32).rearrange("p (i t g) -> p t i g", t=PACK, g=G)
 
-        def separate_x(i):
-            xs[i] = sep.tile([P, 1, PACK, P], F32, name="xs")
-            nc.vector.tensor_copy(out=xs[i][:, 0, :, :].rearrange("p t i -> p i t"), in_=x_words(i)[:, :, :, 2].rearrange("p t i -> p i t"))
-
         def separate(engine_copy, rows, name):
             dst = sep.tile([P, 3, 2, P, 2], BF16, name=name)
             for u in range(2):
@@ -70,8 +68,7 @@ def tile_quadjetresnetblock_pb_t_kernel(tc, x, q2, q1, W3, b3, out):
         def tx_x(i, g):
             xt = pst.tile([P, PACK, P], F32, tag="tr", name="xt")
             for t in range(PACK):
-                src = (x_words(i)[:, t, :, 0], x_words(i)[:, t, :, 1], xs[i][:, 0, t, :])[g]
-                nc.tensor.transpose(xt[:, t, :], src, ident_f[:])
+                nc.tensor.transpose(xt[:, t, :], x_words(i)[:, t, :, g], ident_f[:])
             return xt
 
         def ev_x(engine_copy, i, g, xt):
@@ -102,48 +99,50 @@ def tile_quadjetresnetblock_pb_t_kernel(tc, x, q2, q1, W3, b3, out):
             )
 
         def residual_part(engine, i, o0, o1):
-            part = slice(o0 * G, o1 * G)
             engine.tensor_tensor(
-                out=acc[i][:, part].rearrange("p (o g) -> p o g", g=G),
-                in0=q1_sb[i][:, part].rearrange("p (o g) -> p o g", g=G),
-                in1=b_bc[:, o0:o1].unsqueeze(2).to_broadcast([P, o1 - o0, G]),
+                out=acc[i][:, :, o0:o1],
+                in0=q1_sb[i][:].rearrange("p (o g) -> p g o", g=G)[:, :, o0:o1],
+                in1=b_bc[:, o0:o1].unsqueeze(1).to_broadcast([P, G, o1 - o0]),
                 op=ADD,
             )
 
-        def residual(i):
-            acc[i] = res.tile([P, O * G], F32, name="acc")
+        def residual_v(i):
+            acc[i] = res.tile([P, G, O], F32, name="acc")
             residual_part(nc.vector, i, O_POOL, O)
-            nc.vector.memset(acc[i][:, 0:1], 0.0)
+
+        def residual_g(i):
+            nc.vector.memset(acc[i][:, 0, 0:1], 0.0)
             residual_part(nc.gpsimd, i, 0, O_POOL)
 
-        def mm(i, oc):
-            ps[oc] = psm.tile([P, G, P], F32, tag="mm", name="ps")
-            for g in range(G):
-                for k in range(KW):
-                    pos = 2 * g + k if k < 2 else 6 + g
-                    nc.tensor.matmul_mx(
-                        out=ps[oc][:, g, :],
-                        lhsT=codes[i][:, pos, :].bitcast(FP8X4),
-                        lhsT_scale=scales[i][:, pos, :],
-                        rhs=w_codes[:, k, oc * P:(oc + 1) * P].bitcast(FP8X4),
-                        rhs_scale=w_scales[:, k, oc * P:(oc + 1) * P],
-                        start=(k == 0),
-                        stop=(k == KW - 1),
-                    )
+        def mm(i, g):
+            ps[g] = psm.tile([P, O], F32, tag="mm", name="ps")
+            for k in range(KW):
+                pos = 2 * g + k if k < 2 else 6 + g
+                nc.tensor.matmul_mx(
+                    out=ps[g][:],
+                    lhsT=codes[i][:, pos, :].bitcast(FP8X4),
+                    lhsT_scale=scales[i][:, pos, :],
+                    rhs=w_codes[:, k, :].bitcast(FP8X4),
+                    rhs_scale=w_scales[:, k, :],
+                    start=(k == 0),
+                    stop=(k == KW - 1),
+                )
 
-        def add(i, oc):
-            part = acc[i][:, oc * P * G:(oc + 1) * P * G].rearrange("p (o g) -> p o g", g=G)
-            nc.vector.tensor_tensor(out=part, in0=ps[oc][:].rearrange("p g o -> p o g"), in1=part, op=ADD)
+        def add(i, g):
+            nc.vector.tensor_tensor(out=acc[i][:, g, :], in0=ps[g][:], in1=acc[i][:, g, :], op=ADD)
 
-        def relu_store(i, oc0, oc1):
-            lo, hi = oc0 * P * G, oc1 * P * G
-            part = acc[i][:, lo:hi]
-            nc.scalar.activation(out=part, in_=part, func=RELU)
-            nc.sync.dma_start(out=out_t[i][:, lo:hi], in_=part)
+        def relu_part(on_vector, i, y, o0, o1):
+            src = acc[i][:, :, o0:o1].rearrange("p g o -> p o g")
+            if on_vector:
+                nc.vector.tensor_scalar(out=y[:, o0:o1, :], in0=src, scalar1=0.0, scalar2=None, op0=MAX)
+            else:
+                nc.scalar.activation(out=y[:, o0:o1, :], in_=src, func=RELU)
+
+        def store(i, y, o0, o1):
+            nc.sync.dma_start(out=out_t[i][:, o0 * G:o1 * G], in_=y[:, o0:o1, :].rearrange("p o g -> p (o g)"))
 
         def separate_rows(i):
             qs[i] = separate(nc.vector.tensor_copy, q2_sb[i][:], "qs")
-            separate_x(i)
 
         def turn(i):
             grp[i] = work.tile([P, NPOS, P, PACK], BF16, align_bytes=64, name="grp")
@@ -168,9 +167,9 @@ def tile_quadjetresnetblock_pb_t_kernel(tc, x, q2, q1, W3, b3, out):
             scales[i] = work.tile([P, NPOS, P], U8, align_bytes=64, name="scales")
 
         def multiply(i):
-            for oc in range(OT):
-                mm(i, oc)
-                add(i, oc)
+            for g in range(G):
+                mm(i, g)
+                add(i, g)
 
         w_sb = const.tile([P, 4, C * KW], BF16)
         b_row = const.tile([P, O], BF16)
@@ -189,7 +188,7 @@ def tile_quadjetresnetblock_pb_t_kernel(tc, x, q2, q1, W3, b3, out):
         w_codes = const.tile([P, KW, O], U32, align_bytes=64)
         w_scales = const.tile([P, KW, O], U8, align_bytes=64)
         for d in range(4):
-            ws = separate((nc.vector.tensor_copy, nc.vector.tensor_copy, nc.vector.tensor_copy, nc.vector.tensor_copy)[d], w_sb[:, d, :], "ws")
+            ws = separate((nc.scalar.copy, nc.vector.tensor_copy, nc.vector.tensor_copy, nc.vector.tensor_copy)[d], w_sb[:, d, :], "ws")
             for s0, s1 in ((0, 2), (2, 3)):
                 ev_triples((nc.scalar.copy, nc.scalar.copy, nc.scalar.copy, nc.scalar.copy)[d], grp_words(w_grp)[:, s0:s1, d * P:(d + 1) * P, :], tx_triples(ws, s0, s1))
         separate_rows(0)
@@ -209,7 +208,8 @@ def tile_quadjetresnetblock_pb_t_kernel(tc, x, q2, q1, W3, b3, out):
         separate_rows(1)
         quant(0, 4, 4)
         quant(0, 8, 1)
-        residual(0)
+        residual_v(0)
+        residual_g(0)
         turn(1)
         separate_rows(2)
 
@@ -224,11 +224,19 @@ def tile_quadjetresnetblock_pb_t_kernel(tc, x, q2, q1, W3, b3, out):
             if i + 1 < NT:
                 quant(i + 1, 4, 4)
                 quant(i + 1, 8, 1)
-                residual(i + 1)
+                residual_v(i + 1)
+            if i > 0:
+                y = res.tile([P, O, G], F32, name="y")
+                relu_part(True, i - 1, y, O_RELU, O)
+            if i + 1 < NT:
+                residual_g(i + 1)
             if i + 2 < NT:
                 turn(i + 2)
             multiply(i)
             if i > 0:
-                relu_store(i - 1, 0, OT)
-        for oc0, oc1 in ((0, 2), (2, 3), (3, 4)):
-            relu_store(NT - 1, oc0, oc1)
+                relu_part(False, i - 1, y, 0, O_RELU)
+                store(i - 1, y, 0, O)
+        y = res.tile([P, O, G], F32, name="y")
+        for j, (o0, o1) in enumerate(((0, 128), (128, 320), (320, 384), (384, 512))):
+            relu_part(j % 2 == 1, NT - 1, y, o0, o1)
+            store(NT - 1, y, o0, o1)

from contextlib import ExitStack

import concourse.mybir as mybir
from concourse.masks import make_identity

F32 = mybir.dt.float32
BF16 = mybir.dt.bfloat16
U32 = mybir.dt.uint32
U8 = mybir.dt.uint8
FP8X4 = mybir.dt.float8_e4m3fn_x4
ADD = mybir.AluOpType.add
MAX = mybir.AluOpType.max
RELU = mybir.ActivationFunctionType.Relu

P = 128
N, C, G, KW = 1536, 512, 3, 3
O = 512
NT = N // P
PACK = 4
OT = O // P
NPOS = 9
O_POOL = 320
AHEAD = 5
O_RELU = 448
FLOPS = 2 * N * G * O * C * KW


def tile_quadjetresnetblock_pb_t_kernel(tc, x, q2, q1, W3, b3, out):
    nc = tc.nc
    x_t = x.rearrange("(i p) c j -> i p (c j)", p=P)
    q2_t = q2.rearrange("(i p) c g -> i p (c g)", p=P)
    q1_t = q1.rearrange("(i p) c g -> i p (c g)", p=P)
    out_t = out.rearrange("(i p) o g -> i p (o g)", p=P)
    w_t = W3.rearrange("(d p) c k -> d p (c k)", p=P)

    with ExitStack() as ctx:
        const = ctx.enter_context(tc.tile_pool(name="const", bufs=1))
        xin = ctx.enter_context(tc.tile_pool(name="xin", bufs=AHEAD + 1))
        sep = ctx.enter_context(tc.tile_pool(name="sep", bufs=3))
        work = ctx.enter_context(tc.tile_pool(name="work", bufs=3))
        res = ctx.enter_context(tc.tile_pool(name="res", bufs=4))
        pst = ctx.enter_context(tc.psum_pool(name="pst", bufs=5))
        psm = ctx.enter_context(tc.psum_pool(name="psm", bufs=3))
        ctx.enter_context(tc.manual_schedule())

        x_sb, q2_sb, q1_sb, xs, qs, grp, codes, scales, acc, ps = {}, {}, {}, {}, {}, {}, {}, {}, {}, {}

        def load(i):
            x_sb[i] = xin.tile([P, C * 6], BF16, name="x_sb")
            nc.sync.dma_start(out=x_sb[i][:], in_=x_t[i])
            q2_sb[i] = xin.tile([P, C * G], BF16, name="q2_sb")
            nc.sync.dma_start(out=q2_sb[i][:], in_=q2_t[i])
            q1_sb[i] = xin.tile([P, C * G], BF16, name="q1_sb")
            nc.sync.dma_start(out=q1_sb[i][:], in_=q1_t[i])

        def x_words(i):
            return x_sb[i][:].bitcast(F32).rearrange("p (i t g) -> p t i g", t=PACK, g=G)

        def separate(engine_copy, rows, name):
            dst = sep.tile([P, 3, 2, P, 2], BF16, name=name)
            for u in range(2):
                engine_copy(
                    out=dst[:, :, u, :, :].rearrange("p s i e -> p i e s"),
                    in_=rows.rearrange("p (i u e s) -> p u i e s", u=2, e=2, s=3)[:, u, :, :, :],
                )
            return dst

        def tx_x(i, g):
            xt = pst.tile([P, PACK, P], F32, tag="tr", name="xt")
            for t in range(PACK):
                nc.tensor.transpose(xt[:, t, :], x_words(i)[:, t, :, g], ident_f[:])
            return xt

        def ev_x(engine_copy, i, g, xt):
            engine_copy(
                out=grp[i][:, 2 * g:2 * g + 2, :, :],
                in_=xt[:].rearrange("p t m -> p (t m)").bitcast(BF16).rearrange("p (t m k) -> p k m t", t=PACK, k=2),
            )

        def tx_triples(src, s0, s1):
            words = src[:].rearrange("p s u i e -> p (s u i e)").bitcast(F32).rearrange("p (s u i) -> p s u i", s=3, u=2)
            bank = pst.tile([P, s1 - s0, 2, P], F32, tag="tr", name="bank")
            for s in range(s0, s1):
                for u in range(2):
                    nc.tensor.transpose(bank[:, s - s0, u, :], words[:, s, u, :], ident_f[:])
            return bank

        def ev_triples(engine_copy, dst, bank):
            engine_copy(out=dst, in_=bank[:].rearrange("p s u j -> p s j u"))

        def grp_words(tile):
            return tile[:].rearrange("p a m u -> p (a m u)").bitcast(F32).rearrange("p (a m u) -> p a m u", a=tile.shape[1], u=2)

        def quant(i, p0, npos):
            nc.vector.quantize_mx(
                out=codes[i][:, p0:p0 + npos, :].rearrange("p a m -> p (a m)").bitcast(FP8X4),
                scales=scales[i][:, p0:p0 + npos, :].rearrange("p a m -> p (a m)"),
                in_=grp[i][:, p0:p0 + npos, :, :].rearrange("p a m u -> p (a m u)"),
            )

        def residual_part(engine, i, o0, o1):
            engine.tensor_tensor(
                out=acc[i][:, :, o0:o1],
                in0=q1_sb[i][:].rearrange("p (o g) -> p g o", g=G)[:, :, o0:o1],
                in1=b_bc[:, o0:o1].unsqueeze(1).to_broadcast([P, G, o1 - o0]),
                op=ADD,
            )

        def residual_v(i):
            acc[i] = res.tile([P, G, O], F32, name="acc")
            residual_part(nc.vector, i, O_POOL, O)

        def residual_g(i):
            nc.vector.memset(acc[i][:, 0, 0:1], 0.0)
            residual_part(nc.gpsimd, i, 0, O_POOL)

        def mm(i, g):
            ps[g] = psm.tile([P, O], F32, tag="mm", name="ps")
            for k in range(KW):
                pos = 2 * g + k if k < 2 else 6 + g
                nc.tensor.matmul_mx(
                    out=ps[g][:],
                    lhsT=codes[i][:, pos, :].bitcast(FP8X4),
                    lhsT_scale=scales[i][:, pos, :],
                    rhs=w_codes[:, k, :].bitcast(FP8X4),
                    rhs_scale=w_scales[:, k, :],
                    start=(k == 0),
                    stop=(k == KW - 1),
                )

        def add(i, g):
            nc.vector.tensor_tensor(out=acc[i][:, g, :], in0=ps[g][:], in1=acc[i][:, g, :], op=ADD)

        def relu_part(on_vector, i, y, o0, o1):
            src = acc[i][:, :, o0:o1].rearrange("p g o -> p o g")
            if on_vector:
                nc.vector.tensor_scalar(out=y[:, o0:o1, :], in0=src, scalar1=0.0, scalar2=None, op0=MAX)
            else:
                nc.scalar.activation(out=y[:, o0:o1, :], in_=src, func=RELU)

        def store(i, y, o0, o1):
            nc.sync.dma_start(out=out_t[i][:, o0 * G:o1 * G], in_=y[:, o0:o1, :].rearrange("p o g -> p (o g)"))

        def separate_rows(i):
            qs[i] = separate(nc.vector.tensor_copy, q2_sb[i][:], "qs")

        def turn(i):
            grp[i] = work.tile([P, NPOS, P, PACK], BF16, align_bytes=64, name="grp")
            gw = grp_words(grp[i])
            ev_x(nc.scalar.copy, i, 0, tx_x(i, 0))
            ev_x(nc.scalar.copy, i, 1, tx_x(i, 1))
            ev_x(nc.scalar.copy, i, 2, tx_x(i, 2))
            ev_triples(nc.scalar.copy, gw[:, 6:8, :, :], tx_triples(qs[i], 0, 2))
            ev_triples(nc.scalar.copy, gw[:, 8:9, :, :], tx_triples(qs[i], 2, 3))

        def turn_first(i):
            grp[i] = work.tile([P, NPOS, P, PACK], BF16, align_bytes=64, name="grp")
            gw = grp_words(grp[i])
            ev_x(nc.scalar.copy, i, 0, tx_x(i, 0))
            ev_x(nc.scalar.copy, i, 1, tx_x(i, 1))
            ev_x(nc.scalar.copy, i, 2, tx_x(i, 2))
            ev_triples(nc.scalar.copy, gw[:, 6:8, :, :], tx_triples(qs[i], 0, 2))
            ev_triples(nc.scalar.copy, gw[:, 8:9, :, :], tx_triples(qs[i], 2, 3))

        def open_codes(i):
            codes[i] = work.tile([P, NPOS, P], U32, align_bytes=64, name="codes")
            scales[i] = work.tile([P, NPOS, P], U8, align_bytes=64, name="scales")

        def multiply(i):
            for g in range(G):
                mm(i, g)
                add(i, g)

        w_sb = const.tile([P, 4, C * KW], BF16)
        b_row = const.tile([P, O], BF16)
        nc.vector.memset(b_row[:], 0.0)
        for d in range(4):
            nc.sync.dma_start(out=w_sb[:, d, :], in_=w_t[d])
        nc.sync.dma_start(out=b_row[0:1, :], in_=b3.unsqueeze(0))
        for i in range(AHEAD):
            load(i)
        ident_f = const.tile([P, P], F32)
        make_identity(nc, ident_f[:])
        ones = const.tile([P, P], BF16)
        nc.gpsimd.memset(ones[:], 1.0)

        w_grp = const.tile([P, KW, O, PACK], BF16, align_bytes=64)
        w_codes = const.tile([P, KW, O], U32, align_bytes=64)
        w_scales = const.tile([P, KW, O], U8, align_bytes=64)
        for d in range(4):
            ws = separate((nc.scalar.copy, nc.vector.tensor_copy, nc.vector.tensor_copy, nc.vector.tensor_copy)[d], w_sb[:, d, :], "ws")
            for s0, s1 in ((0, 2), (2, 3)):
                ev_triples((nc.scalar.copy, nc.scalar.copy, nc.scalar.copy, nc.scalar.copy)[d], grp_words(w_grp)[:, s0:s1, d * P:(d + 1) * P, :], tx_triples(ws, s0, s1))
        separate_rows(0)
        turn_first(0)
        for k in range(KW):
            nc.vector.quantize_mx(
                out=w_codes[:, k, :].bitcast(FP8X4),
                scales=w_scales[:, k, :],
                in_=w_grp[:, k, :, :].rearrange("p o u -> p (o u)"),
            )
        b_ps = pst.tile([P, O], F32, tag="tr", name="b_ps")
        nc.tensor.matmul(b_ps[:], ones[:], b_row[:], start=True, stop=True)
        b_bc = const.tile([P, O], BF16)
        nc.scalar.copy(out=b_bc[:], in_=b_ps[:])
        open_codes(0)
        quant(0, 0, 4)
        separate_rows(1)
        quant(0, 4, 4)
        quant(0, 8, 1)
        residual_v(0)
        residual_g(0)
        turn(1)
        separate_rows(2)

        for i in range(NT):
            if i + AHEAD < NT:
                load(i + AHEAD)
            if i + 1 < NT:
                open_codes(i + 1)
                quant(i + 1, 0, 4)
            if i + 3 < NT:
                separate_rows(i + 3)
            if i + 1 < NT:
                quant(i + 1, 4, 4)
                quant(i + 1, 8, 1)
                residual_v(i + 1)
            if i > 0:
                y = res.tile([P, O, G], F32, name="y")
                relu_part(True, i - 1, y, O_RELU, O)
            if i + 1 < NT:
                residual_g(i + 1)
            if i + 2 < NT:
                turn(i + 2)
            multiply(i)
            if i > 0:
                relu_part(False, i - 1, y, 0, O_RELU)
                store(i - 1, y, 0, O)
        y = res.tile([P, O, G], F32, name="y")
        for j, (o0, o1) in enumerate(((0, 128), (128, 320), (320, 384), (384, 512))):
            relu_part(j % 2 == 1, NT - 1, y, o0, o1)
            store(NT - 1, y, o0, o1)
